import numpy as np
import ml_dtypes


def mxq(x, axis, fmt="e4m3"):
    dtype, down = {"e4m3": (ml_dtypes.float8_e4m3fn, 7), "e5m2": (ml_dtypes.float8_e5m2, 14)}[fmt]
    v = np.moveaxis(np.asarray(x, np.float32).astype(ml_dtypes.bfloat16).astype(np.float64), axis, -1)
    blocks = v.reshape(v.shape[:-1] + (-1, 32))
    amax = np.abs(blocks).max(-1, keepdims=True)
    byte = np.maximum(np.where(amax > 0, np.frexp(amax)[1] - 1 + 127, 0) - down, 1)
    scale = np.exp2(byte - 127.0)
    codes = (blocks / scale).astype(np.float32).astype(dtype).astype(np.float64)
    return np.moveaxis((codes * scale).reshape(v.shape), -1, axis)


WIDE = False


def mx_kscale(k):
    if not WIDE:
        return np.ones(k)
    levels = np.array([10, -10, 5, -5, 0])
    a = np.random.permutation(np.resize(levels, k // 512 * 4)).reshape(k // 512, 4)
    idx = np.arange(k)
    return np.exp2(a[idx // 512, idx % 128 // 32])


BF16 = ml_dtypes.bfloat16


def bf(x):
    return np.asarray(x, np.float32).astype(BF16)


def f64(x):
    return np.asarray(x).astype(np.float64)


B, SQ, SK, D, DK, L = 2, 1024, 1024, 1024, 64, 10000
P = max(SQ, SK)


def setup_inputs():
    s, t = mx_kscale(D), mx_kscale(D)
    return {"pe": bf(np.random.standard_normal((P, D)) * s),
            "Uq": bf(np.random.standard_normal((D, D)) * 0.6 / np.sqrt(D) / s[:, None] * t),
            "Uk": bf(np.random.standard_normal((D, D)) * 0.6 / np.sqrt(D) / s[:, None] / t)}


def reference(pe, Uq, Uk):
    peq = mxq(f64(pe), 1, "e4m3")
    q_pe = peq[:SQ] @ mxq(f64(Uq), 0, "e4m3")
    k_pe = peq[:SK] @ mxq(f64(Uk), 0, "e4m3")
    return mxq(q_pe, 1, "e4m3") @ mxq(k_pe, 1, "e4m3").T

@@ -1,0 +1,180 @@
+from contextlib import ExitStack
+
+import concourse.mybir as mybir
+from concourse.masks import make_identity
+
+BF16 = mybir.dt.bfloat16
+F32 = mybir.dt.float32
+U32 = mybir.dt.uint32
+U8 = mybir.dt.uint8
+FP8X4 = mybir.dt.float8_e4m3fn_x4
+
+P = 128
+PACK = 4
+K_PASS = P * PACK
+POS = 1024
+FEAT = 1024
+PASSES = FEAT // K_PASS
+BLOCKS = POS // P
+N_KEYS = 512
+KEY_GROUPS = POS // N_KEYS
+BLOCKS_PER_GROUP = N_KEYS // P
+LAG = 1
+
+FLOPS = 3 * 2 * POS * FEAT * FEAT
+
+
+def load_weight(nc, keep, weight, label):
+    raw = keep.tile([P, PASSES, PACK, FEAT], BF16, name="%s_raw" % label)
+    for g in range(PASSES):
+        rows = weight[g * K_PASS : (g + 1) * K_PASS, :]
+        nc.sync.dma_start(
+            out=raw[:, g, :, :].rearrange("q (u e) c -> q u e c", e=2),
+            in_=rows.rearrange("(u q e) c -> q u e c", q=P, e=2),
+        )
+    return raw
+
+
+def quantise_weight(nc, keep, stage, raw, label):
+    codes = keep.tile([P, PASSES, FEAT], U32, name="%s_codes" % label, align_bytes=64)
+    scales = keep.tile([P, PASSES, FEAT], U8, name="%s_scales" % label, align_bytes=64)
+    grouped_of_pass = []
+    for g in range(PASSES):
+        grouped = stage.tile([P, FEAT, PACK], BF16, tag="w_grouped", name="w_grouped", align_bytes=64)
+        for half in range(2):
+            cols = slice(half * FEAT // 2, (half + 1) * FEAT // 2)
+            nc.vector.tensor_copy(
+                out=grouped[:, cols, :].rearrange("p (c i) t -> p c t i", i=4),
+                in_=raw[:, g, :, cols].rearrange("p t (c i) -> p c t i", i=4),
+            )
+        grouped_of_pass.append(grouped)
+    for g in range(PASSES):
+        nc.vector.quantize_mx(
+            out=codes[:, g, :].bitcast(FP8X4),
+            scales=scales[:, g, :],
+            in_=grouped_of_pass[g][:].rearrange("p c t -> p (c t)"),
+        )
+    return codes, scales
+
+
+def project(nc, psum, weight, pe_mx, block, g2):
+    w_codes, w_scales = weight
+    pe_codes, pe_scales = pe_mx
+    bank = psum.tile([P, PACK, P], F32, tag="proj", name="bank")
+    for t in range(PACK):
+        w_cols = slice((PACK * g2 + t) * P, (PACK * g2 + t + 1) * P)
+        for g in range(PASSES):
+            pe_cols = slice(g * P, (g + 1) * P)
+            nc.tensor.matmul_mx(
+                out=bank[:, t, :],
+                lhsT=w_codes[:, g, w_cols].bitcast(FP8X4),
+                lhsT_scale=w_scales[:, g, w_cols],
+                rhs=pe_codes[:, block, pe_cols].bitcast(FP8X4),
+                rhs_scale=pe_scales[:, block, pe_cols],
+                start=(g == 0),
+                stop=(g == PASSES - 1),
+            )
+    return bank
+
+
+def tile_multiheadattention_tupe_pa_kernel(tc, pe, Uq, Uk, out):
+    nc = tc.nc
+    with ExitStack() as ctx:
+        keep = ctx.enter_context(tc.tile_pool(name="keep", bufs=1))
+        stage = ctx.enter_context(tc.tile_pool(name="stage", bufs=3))
+        proj_psum = ctx.enter_context(tc.psum_pool(name="proj_psum", bufs=4))
+        score_psum = ctx.enter_context(tc.psum_pool(name="score_psum", bufs=4))
+
+        uk_raw = load_weight(nc, keep, Uk, "uk")
+        pe_raw = keep.tile([P, BLOCKS * FEAT], BF16)
+        for pair in range(BLOCKS // 2):
+            nc.sync.dma_start(
+                out=pe_raw[:, 2 * pair * FEAT : 2 * (pair + 1) * FEAT].rearrange("p (r f) -> p r f", r=2),
+                in_=pe[2 * pair * P : 2 * (pair + 1) * P, :].rearrange("(r p) f -> p r f", p=P),
+            )
+        uq_raw = load_weight(nc, keep, Uq, "uq")
+
+        ident = keep.tile([P, P], F32)
+        make_identity(nc, ident[:])
+
+        uk_mx = quantise_weight(nc, keep, stage, uk_raw, "uk")
+
+        pe_words = pe_raw[:].bitcast(F32)
+        pe_grouped = keep.tile([P, BLOCKS * PASSES * P * PACK], BF16, align_bytes=64)
+        pe_grouped_words = pe_grouped[:].bitcast(F32).rearrange(
+            "p (r g c u) -> p r g c u", r=BLOCKS, g=PASSES, c=P
+        )
+        pe_codes = keep.tile([P, BLOCKS, PASSES * P], U32, align_bytes=64)
+        pe_scales = keep.tile([P, BLOCKS, PASSES * P], U8, align_bytes=64)
+        words_per_block = FEAT // 2
+        for r in range(BLOCKS):
+            flipped = proj_psum.tile([P, PACK, P], F32, tag="proj", name="flipped")
+            for w in range(PACK):
+                first = r * words_per_block + w * P
+                nc.tensor.transpose(flipped[:, w, :], pe_words[:, first : first + P], ident[:])
+            nc.scalar.copy(
+                out=pe_grouped_words[:, r, :, :, :],
+                in_=flipped[:].rearrange("p (g u) c -> p g c u", u=2),
+            )
+        block_cols = PASSES * P * PACK
+        for r in range(BLOCKS):
+            nc.vector.quantize_mx(
+                out=pe_codes[:, r, :].bitcast(FP8X4),
+                scales=pe_scales[:, r, :],
+                in_=pe_grouped[:, r * block_cols : (r + 1) * block_cols],
+            )
+        pe_mx = (pe_codes, pe_scales)
+
+        uq_mx = quantise_weight(nc, keep, stage, uq_raw, "uq")
+
+        k_codes = keep.tile([P, KEY_GROUPS, PASSES, N_KEYS], U32, align_bytes=64)
+        k_scales = keep.tile([P, KEY_GROUPS, PASSES, N_KEYS], U8, align_bytes=64)
+        for h in range(KEY_GROUPS):
+            for g2 in range(PASSES):
+                k_grouped = stage.tile([P, N_KEYS, PACK], BF16, align_bytes=64)
+                for i in range(BLOCKS_PER_GROUP):
+                    bank = project(nc, proj_psum, uk_mx, pe_mx, h * BLOCKS_PER_GROUP + i, g2)
+                    nc.scalar.copy(
+                        out=k_grouped[:, i * P : (i + 1) * P, :],
+                        in_=bank[:].rearrange("p t c -> p c t"),
+                    )
+                nc.vector.quantize_mx(
+                    out=k_codes[:, h, g2, :].bitcast(FP8X4),
+                    scales=k_scales[:, h, g2, :],
+                    in_=k_grouped[:].rearrange("p c t -> p (c t)"),
+                )
+
+        q_codes = keep.tile([P, BLOCKS, PASSES * P], U32, align_bytes=64)
+        q_scales = keep.tile([P, BLOCKS, PASSES * P], U8, align_bytes=64)
+        for step in range(BLOCKS + LAG):
+            if step < BLOCKS:
+                q_grouped = stage.tile([P, PASSES, P, PACK], BF16, align_bytes=64)
+                for g2 in range(PASSES):
+                    bank = project(nc, proj_psum, uq_mx, pe_mx, step, g2)
+                    nc.scalar.copy(
+                        out=q_grouped[:, g2, :, :],
+                        in_=bank[:].rearrange("p t c -> p c t"),
+                    )
+                nc.vector.quantize_mx(
+                    out=q_codes[:, step, :].bitcast(FP8X4),
+                    scales=q_scales[:, step, :],
+                    in_=q_grouped[:].rearrange("p g c t -> p (g c t)"),
+                )
+            if step >= LAG:
+                n = step - LAG
+                rows = stage.tile([P, POS], F32)
+                for h in range(KEY_GROUPS):
+                    scores = score_psum.tile([P, N_KEYS], F32)
+                    for g2 in range(PASSES):
+                        q_cols = slice(g2 * P, (g2 + 1) * P)
+                        nc.tensor.matmul_mx(
+                            out=scores[:],
+                            lhsT=q_codes[:, n, q_cols].bitcast(FP8X4),
+                            lhsT_scale=q_scales[:, n, q_cols],
+                            rhs=k_codes[:, h, g2, :].bitcast(FP8X4),
+                            rhs_scale=k_scales[:, h, g2, :],
+                            start=(g2 == 0),
+                            stop=(g2 == PASSES - 1),
+                        )
+                    nc.vector.tensor_copy(out=rows[:, h * N_KEYS : (h + 1) * N_KEYS], in_=scores[:])
+                nc.sync.dma_start(out=out[n * P : (n + 1) * P, :], in_=rows[:])

@@ -16,88 +16,109 @@ POS = 1024
 FEAT = 1024
 PASSES = FEAT // K_PASS
 BLOCKS = POS // P
-N_KEYS = 512
-KEY_GROUPS = POS // N_KEYS
-BLOCKS_PER_GROUP = N_KEYS // P
+GROUP = 512
+GROUPS = POS // GROUP
+BLOCKS_PER_GROUP = GROUP // P
 LAG = 1
 
 FLOPS = 3 * 2 * POS * FEAT * FEAT
 
 
-def load_weight(nc, keep, weight, label):
-    raw = keep.tile([P, PASSES, PACK, FEAT], BF16, name="%s_raw" % label)
-    for g in range(PASSES):
-        rows = weight[g * K_PASS : (g + 1) * K_PASS, :]
-        nc.sync.dma_start(
-            out=raw[:, g, :, :].rearrange("q (u e) c -> q u e c", e=2),
-            in_=rows.rearrange("(u q e) c -> q u e c", q=P, e=2),
-        )
-    return raw
+def new_side(keep, label):
+    return {
+        "raw": keep.tile([P, PASSES, PASSES, PACK, K_PASS], BF16, name="%s_raw" % label),
+        "w_codes": keep.tile([P, PASSES, PASSES, K_PASS], U32, name="%s_w_codes" % label, align_bytes=64),
+        "w_scales": keep.tile([P, PASSES, PASSES, K_PASS], U8, name="%s_w_scales" % label, align_bytes=64),
+        "codes": keep.tile([P, PASSES, POS], U32, name="%s_codes" % label, align_bytes=64),
+        "scales": keep.tile([P, PASSES, POS], U8, name="%s_scales" % label, align_bytes=64),
+    }
 
 
-def quantise_weight(nc, keep, stage, raw, label):
-    codes = keep.tile([P, PASSES, FEAT], U32, name="%s_codes" % label, align_bytes=64)
-    scales = keep.tile([P, PASSES, FEAT], U8, name="%s_scales" % label, align_bytes=64)
-    grouped_of_pass = []
+def load_weight_half(nc, side, weight, g2):
+    cols = slice(g2 * K_PASS, (g2 + 1) * K_PASS)
     for g in range(PASSES):
-        grouped = stage.tile([P, FEAT, PACK], BF16, tag="w_grouped", name="w_grouped", align_bytes=64)
-        for half in range(2):
-            cols = slice(half * FEAT // 2, (half + 1) * FEAT // 2)
-            nc.vector.tensor_copy(
-                out=grouped[:, cols, :].rearrange("p (c i) t -> p c t i", i=4),
-                in_=raw[:, g, :, cols].rearrange("p t (c i) -> p c t i", i=4),
+        for u in range(2):
+            first = g * K_PASS + u * 2 * P
+            nc.sync.dma_start(
+                out=side["raw"][:, g2, g, 2 * u : 2 * u + 2, :],
+                in_=weight[first : first + 2 * P, cols].rearrange("(p e) c -> p e c", e=2),
             )
-        grouped_of_pass.append(grouped)
+
+
+def quantise_weight_half(nc, stage, side, g2):
+    grouped = stage.tile([P, PASSES, K_PASS, PACK], BF16, align_bytes=64)
+    for g in range(PASSES):
+        nc.vector.tensor_copy(
+            out=grouped[:, g, :, :].rearrange("p (c i) t -> p c t i", i=4),
+            in_=side["raw"][:, g2, g, :, :].rearrange("p t (c i) -> p c t i", i=4),
+        )
     for g in range(PASSES):
         nc.vector.quantize_mx(
-            out=codes[:, g, :].bitcast(FP8X4),
-            scales=scales[:, g, :],
-            in_=grouped_of_pass[g][:].rearrange("p c t -> p (c t)"),
+            out=side["w_codes"][:, g2, g, :].bitcast(FP8X4),
+            scales=side["w_scales"][:, g2, g, :],
+            in_=grouped[:, g, :, :].rearrange("p c t -> p (c t)"),
         )
-    return codes, scales
 
 
-def project(nc, psum, weight, pe_mx, block, g2):
-    w_codes, w_scales = weight
+def project(nc, psum, stage, side, pe_mx, g2, first_block, n_blocks):
     pe_codes, pe_scales = pe_mx
-    bank = psum.tile([P, PACK, P], F32, tag="proj", name="bank")
-    for t in range(PACK):
-        w_cols = slice((PACK * g2 + t) * P, (PACK * g2 + t + 1) * P)
-        for g in range(PASSES):
-            pe_cols = slice(g * P, (g + 1) * P)
-            nc.tensor.matmul_mx(
-                out=bank[:, t, :],
-                lhsT=w_codes[:, g, w_cols].bitcast(FP8X4),
-                lhsT_scale=w_scales[:, g, w_cols],
-                rhs=pe_codes[:, block, pe_cols].bitcast(FP8X4),
-                rhs_scale=pe_scales[:, block, pe_cols],
-                start=(g == 0),
-                stop=(g == PASSES - 1),
-            )
-    return bank
+    grouped = stage.tile([P, n_blocks * P, PACK], BF16, tag="a_grouped%d" % n_blocks, name="a_grouped", align_bytes=64)
+    for i in range(n_blocks):
+        block = first_block + i
+        bank = psum.tile([P, PACK, P], F32, tag="bank", name="proj")
+        for t in range(PACK):
+            w_cols = slice(t * P, (t + 1) * P)
+            for g in range(PASSES):
+                pe_cols = slice(g * P, (g + 1) * P)
+                nc.tensor.matmul_mx(
+                    out=bank[:, t, :],
+                    lhsT=side["w_codes"][:, g2, g, w_cols].bitcast(FP8X4),
+                    lhsT_scale=side["w_scales"][:, g2, g, w_cols],
+                    rhs=pe_codes[:, block, pe_cols].bitcast(FP8X4),
+                    rhs_scale=pe_scales[:, block, pe_cols],
+                    start=(g == 0),
+                    stop=(g == PASSES - 1),
+                )
+        nc.scalar.copy(out=grouped[:, i * P : (i + 1) * P, :], in_=bank[:].rearrange("p t c -> p c t"))
+    return grouped
+
+
+def quantise_projection(nc, side, grouped, g2, first_block, n_blocks):
+    cols = slice(first_block * P, (first_block + n_blocks) * P)
+    nc.vector.quantize_mx(
+        out=side["codes"][:, g2, cols].bitcast(FP8X4),
+        scales=side["scales"][:, g2, cols],
+        in_=grouped[:].rearrange("p c t -> p (c t)"),
+    )
 
 
 def tile_multiheadattention_tupe_pa_kernel(tc, pe, Uq, Uk, out):
     nc = tc.nc
     with ExitStack() as ctx:
         keep = ctx.enter_context(tc.tile_pool(name="keep", bufs=1))
-        stage = ctx.enter_context(tc.tile_pool(name="stage", bufs=3))
-        proj_psum = ctx.enter_context(tc.psum_pool(name="proj_psum", bufs=4))
-        score_psum = ctx.enter_context(tc.psum_pool(name="score_psum", bufs=4))
+        w_stage = ctx.enter_context(tc.tile_pool(name="w_stage", bufs=2))
+        a_stage = ctx.enter_context(tc.tile_pool(name="a_stage", bufs=3))
+        rows_pool = ctx.enter_context(tc.tile_pool(name="rows_pool", bufs=3))
+        psum = ctx.enter_context(tc.psum_pool(name="psum", bufs=8))
 
-        uk_raw = load_weight(nc, keep, Uk, "uk")
+        k_side = new_side(keep, "k")
+        q_side = new_side(keep, "q")
+        load_weight_half(nc, k_side, Uk, 0)
         pe_raw = keep.tile([P, BLOCKS * FEAT], BF16)
         for pair in range(BLOCKS // 2):
             nc.sync.dma_start(
                 out=pe_raw[:, 2 * pair * FEAT : 2 * (pair + 1) * FEAT].rearrange("p (r f) -> p r f", r=2),
                 in_=pe[2 * pair * P : 2 * (pair + 1) * P, :].rearrange("(r p) f -> p r f", p=P),
             )
-        uq_raw = load_weight(nc, keep, Uq, "uq")
+        load_weight_half(nc, k_side, Uk, 1)
+        load_weight_half(nc, q_side, Uq, 0)
+        load_weight_half(nc, q_side, Uq, 1)
 
         ident = keep.tile([P, P], F32)
         make_identity(nc, ident[:])
 
-        uk_mx = quantise_weight(nc, keep, stage, uk_raw, "uk")
+        halves = [(k_side, 0), (k_side, 1), (q_side, 0), (q_side, 1)]
+        quantise_weight_half(nc, w_stage, k_side, 0)
 
         pe_words = pe_raw[:].bitcast(F32)
         pe_grouped = keep.tile([P, BLOCKS * PASSES * P * PACK], BF16, align_bytes=64)
@@ -106,9 +127,11 @@ def tile_multiheadattention_tupe_pa_kernel(tc, pe, Uq, Uk, out):
         )
         pe_codes = keep.tile([P, BLOCKS, PASSES * P], U32, align_bytes=64)
         pe_scales = keep.tile([P, BLOCKS, PASSES * P], U8, align_bytes=64)
+        pe_mx = (pe_codes, pe_scales)
         words_per_block = FEAT // 2
+        block_cols = PASSES * P * PACK
         for r in range(BLOCKS):
-            flipped = proj_psum.tile([P, PACK, P], F32, tag="proj", name="flipped")
+            flipped = psum.tile([P, PACK, P], F32, tag="bank", name="flipped")
             for w in range(PACK):
                 first = r * words_per_block + w * P
                 nc.tensor.transpose(flipped[:, w, :], pe_words[:, first : first + P], ident[:])
@@ -116,65 +139,42 @@ def tile_multiheadattention_tupe_pa_kernel(tc, pe, Uq, Uk, out):
                 out=pe_grouped_words[:, r, :, :, :],
                 in_=flipped[:].rearrange("p (g u) c -> p g c u", u=2),
             )
-        block_cols = PASSES * P * PACK
-        for r in range(BLOCKS):
             nc.vector.quantize_mx(
                 out=pe_codes[:, r, :].bitcast(FP8X4),
                 scales=pe_scales[:, r, :],
                 in_=pe_grouped[:, r * block_cols : (r + 1) * block_cols],
             )
-        pe_mx = (pe_codes, pe_scales)
 
-        uq_mx = quantise_weight(nc, keep, stage, uq_raw, "uq")
+        for s in range(len(halves) - 1):
+            side, g2 = halves[s]
+            for h in range(GROUPS):
+                grouped = project(nc, psum, a_stage, side, pe_mx, g2, h * BLOCKS_PER_GROUP, BLOCKS_PER_GROUP)
+                if h == 0:
+                    quantise_weight_half(nc, w_stage, halves[s + 1][0], halves[s + 1][1])
+                quantise_projection(nc, side, grouped, g2, h * BLOCKS_PER_GROUP, BLOCKS_PER_GROUP)
 
-        k_codes = keep.tile([P, KEY_GROUPS, PASSES, N_KEYS], U32, align_bytes=64)
-        k_scales = keep.tile([P, KEY_GROUPS, PASSES, N_KEYS], U8, align_bytes=64)
-        for h in range(KEY_GROUPS):
-            for g2 in range(PASSES):
-                k_grouped = stage.tile([P, N_KEYS, PACK], BF16, align_bytes=64)
-                for i in range(BLOCKS_PER_GROUP):
-                    bank = project(nc, proj_psum, uk_mx, pe_mx, h * BLOCKS_PER_GROUP + i, g2)
-                    nc.scalar.copy(
-                        out=k_grouped[:, i * P : (i + 1) * P, :],
-                        in_=bank[:].rearrange("p t c -> p c t"),
-                    )
-                nc.vector.quantize_mx(
-                    out=k_codes[:, h, g2, :].bitcast(FP8X4),
-                    scales=k_scales[:, h, g2, :],
-                    in_=k_grouped[:].rearrange("p c t -> p (c t)"),
-                )
-
-        q_codes = keep.tile([P, BLOCKS, PASSES * P], U32, align_bytes=64)
-        q_scales = keep.tile([P, BLOCKS, PASSES * P], U8, align_bytes=64)
         for step in range(BLOCKS + LAG):
             if step < BLOCKS:
-                q_grouped = stage.tile([P, PASSES, P, PACK], BF16, align_bytes=64)
-                for g2 in range(PASSES):
-                    bank = project(nc, proj_psum, uq_mx, pe_mx, step, g2)
-                    nc.scalar.copy(
-                        out=q_grouped[:, g2, :, :],
-                        in_=bank[:].rearrange("p t c -> p c t"),
-                    )
-                nc.vector.quantize_mx(
-                    out=q_codes[:, step, :].bitcast(FP8X4),
-                    scales=q_scales[:, step, :],
-                    in_=q_grouped[:].rearrange("p g c t -> p (g c t)"),
-                )
+                grouped = project(nc, psum, a_stage, q_side, pe_mx, 1, step, 1)
+                quantise_projection(nc, q_side, grouped, 1, step, 1)
             if step >= LAG:
                 n = step - LAG
-                rows = stage.tile([P, POS], F32)
-                for h in range(KEY_GROUPS):
-                    scores = score_psum.tile([P, N_KEYS], F32)
+                for h in range(GROUPS):
+                    scores = psum.tile([P, GROUP], F32, tag="bank", name="scores")
+                    keys = slice(h * GROUP, (h + 1) * GROUP)
                     for g2 in range(PASSES):
-                        q_cols = slice(g2 * P, (g2 + 1) * P)
                         nc.tensor.matmul_mx(
                             out=scores[:],
-                            lhsT=q_codes[:, n, q_cols].bitcast(FP8X4),
-                            lhsT_scale=q_scales[:, n, q_cols],
-                            rhs=k_codes[:, h, g2, :].bitcast(FP8X4),
-                            rhs_scale=k_scales[:, h, g2, :],
+                            lhsT=q_side["codes"][:, g2, n * P : (n + 1) * P].bitcast(FP8X4),
+                            lhsT_scale=q_side["scales"][:, g2, n * P : (n + 1) * P],
+                            rhs=k_side["codes"][:, g2, keys].bitcast(FP8X4),
+                            rhs_scale=k_side["scales"][:, g2, keys],
                             start=(g2 == 0),
                             stop=(g2 == PASSES - 1),
                         )
-                    nc.vector.tensor_copy(out=rows[:, h * N_KEYS : (h + 1) * N_KEYS], in_=scores[:])
-                nc.sync.dma_start(out=out[n * P : (n + 1) * P, :], in_=rows[:])
+                    rows = rows_pool.tile([P, GROUP], F32, tag="rows%d" % (h % 2), name="rows")
+                    if h % 2 == 0:
+                        nc.vector.tensor_copy(out=rows[:], in_=scores[:])
+                    else:
+                        nc.scalar.copy(out=rows[:], in_=scores[:])
+                    nc.sync.dma_start(out=out[n * P : (n + 1) * P, keys], in_=rows[:])

@@ -95,6 +95,7 @@ def quantise_projection(nc, side, grouped, g2, first_block, n_blocks):
 def tile_multiheadattention_tupe_pa_kernel(tc, pe, Uq, Uk, out):
     nc = tc.nc
     with ExitStack() as ctx:
+        ctx.enter_context(tc.manual_schedule())
         keep = ctx.enter_context(tc.tile_pool(name="keep", bufs=1))
         w_stage = ctx.enter_context(tc.tile_pool(name="w_stage", bufs=2))
         a_stage = ctx.enter_context(tc.tile_pool(name="a_stage", bufs=3))

@@ -19,7 +19,7 @@ BLOCKS = POS // P
 GROUP = 512
 GROUPS = POS // GROUP
 BLOCKS_PER_GROUP = GROUP // P
-LAG = 1
+LAG = 2
 
 FLOPS = 3 * 2 * POS * FEAT * FEAT
 
@@ -98,7 +98,7 @@ def tile_multiheadattention_tupe_pa_kernel(tc, pe, Uq, Uk, out):
         ctx.enter_context(tc.manual_schedule())
         keep = ctx.enter_context(tc.tile_pool(name="keep", bufs=1))
         w_stage = ctx.enter_context(tc.tile_pool(name="w_stage", bufs=2))
-        a_stage = ctx.enter_context(tc.tile_pool(name="a_stage", bufs=3))
+        a_stage = ctx.enter_context(tc.tile_pool(name="a_stage", bufs=6))
         rows_pool = ctx.enter_context(tc.tile_pool(name="rows_pool", bufs=3))
         psum = ctx.enter_context(tc.psum_pool(name="psum", bufs=8))
 
@@ -146,12 +146,13 @@ def tile_multiheadattention_tupe_pa_kernel(tc, pe, Uq, Uk, out):
                 in_=pe_grouped[:, r * block_cols : (r + 1) * block_cols],
             )
 
+        for side, g2 in halves[1:]:
+            quantise_weight_half(nc, w_stage, side, g2)
+
         for s in range(len(halves) - 1):
             side, g2 = halves[s]
             for h in range(GROUPS):
                 grouped = project(nc, psum, a_stage, side, pe_mx, g2, h * BLOCKS_PER_GROUP, BLOCKS_PER_GROUP)
-                if h == 0:
-                    quantise_weight_half(nc, w_stage, halves[s + 1][0], halves[s + 1][1])
                 quantise_projection(nc, side, grouped, g2, h * BLOCKS_PER_GROUP, BLOCKS_PER_GROUP)
 
         for step in range(BLOCKS + LAG):

@@ -19,7 +19,11 @@ BLOCKS = POS // P
 GROUP = 512
 GROUPS = POS // GROUP
 BLOCKS_PER_GROUP = GROUP // P
-LAG = 2
+LEAD = 4
+C0_AFTER = 5
+C1_AFTER = 7
+S_SHARE2 = 128
+S_AT = 3
 
 FLOPS = 3 * 2 * POS * FEAT * FEAT
 
@@ -45,42 +49,46 @@ def load_weight_half(nc, side, weight, g2):
             )
 
 
+def lay_out_weight(engine_copy, side, grouped, g2, g, c0, c1):
+    engine_copy(
+        out=grouped[:, g, c0:c1, :].rearrange("p (c i) t -> p c t i", i=4),
+        in_=side["raw"][:, g2, g, :, c0:c1].rearrange("p t (c i) -> p c t i", i=4),
+    )
+
+
+def quantise_weight(nc, side, grouped, g2, g):
+    nc.vector.quantize_mx(
+        out=side["w_codes"][:, g2, g, :].bitcast(FP8X4),
+        scales=side["w_scales"][:, g2, g, :],
+        in_=grouped[:, g, :, :].rearrange("p c t -> p (c t)"),
+    )
+
+
 def quantise_weight_half(nc, stage, side, g2):
-    grouped = stage.tile([P, PASSES, K_PASS, PACK], BF16, align_bytes=64)
+    grouped = stage.tile([P, PASSES, K_PASS, PACK], BF16, name="w_grouped", align_bytes=64)
     for g in range(PASSES):
-        nc.vector.tensor_copy(
-            out=grouped[:, g, :, :].rearrange("p (c i) t -> p c t i", i=4),
-            in_=side["raw"][:, g2, g, :, :].rearrange("p t (c i) -> p c t i", i=4),
-        )
+        lay_out_weight(nc.vector.tensor_copy, side, grouped, g2, g, 0, K_PASS)
     for g in range(PASSES):
-        nc.vector.quantize_mx(
-            out=side["w_codes"][:, g2, g, :].bitcast(FP8X4),
-            scales=side["w_scales"][:, g2, g, :],
-            in_=grouped[:, g, :, :].rearrange("p c t -> p (c t)"),
-        )
+        quantise_weight(nc, side, grouped, g2, g)
 
 
-def project(nc, psum, stage, side, pe_mx, g2, first_block, n_blocks):
+def project_block(nc, psum, side, pe_mx, g2, block, grouped, i, copy):
     pe_codes, pe_scales = pe_mx
-    grouped = stage.tile([P, n_blocks * P, PACK], BF16, tag="a_grouped%d" % n_blocks, name="a_grouped", align_bytes=64)
-    for i in range(n_blocks):
-        block = first_block + i
-        bank = psum.tile([P, PACK, P], F32, tag="bank", name="proj")
-        for t in range(PACK):
-            w_cols = slice(t * P, (t + 1) * P)
-            for g in range(PASSES):
-                pe_cols = slice(g * P, (g + 1) * P)
-                nc.tensor.matmul_mx(
-                    out=bank[:, t, :],
-                    lhsT=side["w_codes"][:, g2, g, w_cols].bitcast(FP8X4),
-                    lhsT_scale=side["w_scales"][:, g2, g, w_cols],
-                    rhs=pe_codes[:, block, pe_cols].bitcast(FP8X4),
-                    rhs_scale=pe_scales[:, block, pe_cols],
-                    start=(g == 0),
-                    stop=(g == PASSES - 1),
-                )
-        nc.scalar.copy(out=grouped[:, i * P : (i + 1) * P, :], in_=bank[:].rearrange("p t c -> p c t"))
-    return grouped
+    bank = psum.tile([P, PACK, P], F32, tag="bank", name="proj")
+    for t in range(PACK):
+        w_cols = slice(t * P, (t + 1) * P)
+        for g in range(PASSES):
+            pe_cols = slice(g * P, (g + 1) * P)
+            nc.tensor.matmul_mx(
+                out=bank[:, t, :],
+                lhsT=side["w_codes"][:, g2, g, w_cols].bitcast(FP8X4),
+                lhsT_scale=side["w_scales"][:, g2, g, w_cols],
+                rhs=pe_codes[:, block, pe_cols].bitcast(FP8X4),
+                rhs_scale=pe_scales[:, block, pe_cols],
+                start=(g == 0),
+                stop=(g == PASSES - 1),
+            )
+    copy(out=grouped[:, i * P : (i + 1) * P, :], in_=bank[:].rearrange("p t c -> p c t"))
 
 
 def quantise_projection(nc, side, grouped, g2, first_block, n_blocks):
@@ -119,7 +127,12 @@ def tile_multiheadattention_tupe_pa_kernel(tc, pe, Uq, Uk, out):
         make_identity(nc, ident[:])
 
         halves = [(k_side, 0), (k_side, 1), (q_side, 0), (q_side, 1)]
-        quantise_weight_half(nc, w_stage, k_side, 0)
+
+        first = w_stage.tile([P, PASSES, K_PASS, PACK], BF16, name="w_grouped", align_bytes=64)
+        lay_out_weight(nc.vector.tensor_copy, k_side, first, 0, 0, 0, K_PASS)
+        lay_out_weight(nc.vector.tensor_copy, k_side, first, 0, 1, 0, K_PASS)
+        quantise_weight(nc, k_side, first, 0, 0)
+        quantise_weight(nc, k_side, first, 0, 1)
 
         pe_words = pe_raw[:].bitcast(F32)
         pe_grouped = keep.tile([P, BLOCKS * PASSES * P * PACK], BF16, align_bytes=64)
@@ -131,11 +144,12 @@ def tile_multiheadattention_tupe_pa_kernel(tc, pe, Uq, Uk, out):
         pe_mx = (pe_codes, pe_scales)
         words_per_block = FEAT // 2
         block_cols = PASSES * P * PACK
-        for r in range(BLOCKS):
+
+        def flip(r):
             flipped = psum.tile([P, PACK, P], F32, tag="bank", name="flipped")
             for w in range(PACK):
-                first = r * words_per_block + w * P
-                nc.tensor.transpose(flipped[:, w, :], pe_words[:, first : first + P], ident[:])
+                start = r * words_per_block + w * P
+                nc.tensor.transpose(flipped[:, w, :], pe_words[:, start : start + P], ident[:])
             nc.scalar.copy(
                 out=pe_grouped_words[:, r, :, :, :],
                 in_=flipped[:].rearrange("p (g u) c -> p g c u", u=2),
@@ -146,37 +160,75 @@ def tile_multiheadattention_tupe_pa_kernel(tc, pe, Uq, Uk, out):
                 in_=pe_grouped[:, r * block_cols : (r + 1) * block_cols],
             )
 
-        for side, g2 in halves[1:]:
-            quantise_weight_half(nc, w_stage, side, g2)
+        grouped_of = {}
 
-        for s in range(len(halves) - 1):
+        def project(s, block):
+            side, g2 = halves[s]
+            h, i = divmod(block, BLOCKS_PER_GROUP)
+            if i == 0:
+                grouped_of[(s, h)] = a_stage.tile([P, GROUP, PACK], BF16, tag="a_grouped4", name="a_grouped", align_bytes=64)
+            project_block(nc, psum, side, pe_mx, g2, block, grouped_of[(s, h)], i, nc.scalar.copy)
+
+        second = w_stage.tile([P, PASSES, K_PASS, PACK], BF16, name="w_grouped", align_bytes=64)
+        for r in range(BLOCKS):
+            flip(r)
+            if r == C0_AFTER:
+                lay_out_weight(nc.vector.tensor_copy, k_side, second, 1, 0, 0, K_PASS)
+            if r == C1_AFTER:
+                lay_out_weight(nc.vector.tensor_copy, k_side, second, 1, 1, 0, K_PASS - S_SHARE2)
+        for block in range(S_AT):
+            project(0, block)
+        lay_out_weight(nc.scalar.copy, k_side, second, 1, 1, K_PASS - S_SHARE2, K_PASS)
+        quantise_weight(nc, k_side, second, 1, 0)
+        quantise_weight(nc, k_side, second, 1, 1)
+        for side, g2 in halves[2:]:
+            quantise_weight_half(nc, w_stage, side, g2)
+        for block in range(S_AT, BLOCKS):
+            project(0, block)
+        for h in range(GROUPS):
+            quantise_projection(nc, k_side, grouped_of[(0, h)], 0, h * BLOCKS_PER_GROUP, BLOCKS_PER_GROUP)
+        for s in (1, 2):
             side, g2 = halves[s]
             for h in range(GROUPS):
-                grouped = project(nc, psum, a_stage, side, pe_mx, g2, h * BLOCKS_PER_GROUP, BLOCKS_PER_GROUP)
-                quantise_projection(nc, side, grouped, g2, h * BLOCKS_PER_GROUP, BLOCKS_PER_GROUP)
+                for i in range(BLOCKS_PER_GROUP):
+                    project(s, h * BLOCKS_PER_GROUP + i)
+                if (s, h) != (2, 1):
+                    quantise_projection(nc, side, grouped_of[(s, h)], g2, h * BLOCKS_PER_GROUP, BLOCKS_PER_GROUP)
 
-        for step in range(BLOCKS + LAG):
-            if step < BLOCKS:
-                grouped = project(nc, psum, a_stage, q_side, pe_mx, 1, step, 1)
-                quantise_projection(nc, q_side, grouped, 1, step, 1)
-            if step >= LAG:
-                n = step - LAG
-                for h in range(GROUPS):
-                    scores = psum.tile([P, GROUP], F32, tag="bank", name="scores")
-                    keys = slice(h * GROUP, (h + 1) * GROUP)
-                    for g2 in range(PASSES):
-                        nc.tensor.matmul_mx(
-                            out=scores[:],
-                            lhsT=q_side["codes"][:, g2, n * P : (n + 1) * P].bitcast(FP8X4),
-                            lhsT_scale=q_side["scales"][:, g2, n * P : (n + 1) * P],
-                            rhs=k_side["codes"][:, g2, keys].bitcast(FP8X4),
-                            rhs_scale=k_side["scales"][:, g2, keys],
-                            start=(g2 == 0),
-                            stop=(g2 == PASSES - 1),
-                        )
-                    rows = rows_pool.tile([P, GROUP], F32, tag="rows%d" % (h % 2), name="rows")
-                    if h % 2 == 0:
-                        nc.vector.tensor_copy(out=rows[:], in_=scores[:])
-                    else:
-                        nc.scalar.copy(out=rows[:], in_=scores[:])
-                    nc.sync.dma_start(out=out[n * P : (n + 1) * P, keys], in_=rows[:])
+        def last_projection(n):
+            grouped = a_stage.tile([P, P, PACK], BF16, tag="a_grouped1", name="a_grouped", align_bytes=64)
+            project_block(nc, psum, q_side, pe_mx, 1, n, grouped, 0, nc.scalar.copy)
+            quantise_projection(nc, q_side, grouped, 1, n, 1)
+
+        def score(n):
+            for h in range(GROUPS):
+                scores = psum.tile([P, GROUP], F32, tag="bank", name="scores")
+                keys = slice(h * GROUP, (h + 1) * GROUP)
+                for g2 in range(PASSES):
+                    nc.tensor.matmul_mx(
+                        out=scores[:],
+                        lhsT=q_side["codes"][:, g2, n * P : (n + 1) * P].bitcast(FP8X4),
+                        lhsT_scale=q_side["scales"][:, g2, n * P : (n + 1) * P],
+                        rhs=k_side["codes"][:, g2, keys].bitcast(FP8X4),
+                        rhs_scale=k_side["scales"][:, g2, keys],
+                        start=(g2 == 0),
+                        stop=(g2 == PASSES - 1),
+                    )
+                rows = rows_pool.tile([P, GROUP], F32, tag="rows%d" % (h % 2), name="rows")
+                if h % 2 == 0:
+                    nc.vector.tensor_copy(out=rows[:], in_=scores[:])
+                else:
+                    nc.scalar.copy(out=rows[:], in_=scores[:])
+                nc.sync.dma_start(out=out[n * P : (n + 1) * P, keys], in_=rows[:])
+
+        for n in range(LEAD):
+            last_projection(n)
+        scored = 0
+        for n in range(LEAD, BLOCKS + 1):
+            for i in range(min(2, n - scored - 1) if n < BLOCKS else BLOCKS - scored):
+                score(scored)
+                if scored == 0:
+                    quantise_projection(nc, q_side, grouped_of[(2, 1)], 0, BLOCKS_PER_GROUP, BLOCKS_PER_GROUP)
+                scored += 1
+            if n < BLOCKS:
+                last_projection(n)

@@ -24,6 +24,8 @@ C0_AFTER = 5
 C1_AFTER = 7
 S_SHARE2 = 128
 S_AT = 3
+IDLE_WARMERS = 6
+PIECE_WARMERS = 2
 
 FLOPS = 3 * 2 * POS * FEAT * FEAT
 
@@ -127,6 +129,22 @@ def tile_multiheadattention_tupe_pa_kernel(tc, pe, Uq, Uk, out):
         make_identity(nc, ident[:])
 
         halves = [(k_side, 0), (k_side, 1), (q_side, 0), (q_side, 1)]
+
+        zeros = keep.tile([P, GROUP], BF16)
+        nc.vector.memset(zeros[:], 0.0)
+        wasted = psum.tile([P, GROUP], F32, tag="bank", name="wasted")
+        for i in range(IDLE_WARMERS):
+            nc.tensor.matmul(out=wasted[:], lhsT=zeros[:, :P], rhs=zeros[:], start=True, stop=True)
+        for g in range(PASSES):
+            for u in range(2):
+                for i in range(PIECE_WARMERS):
+                    nc.tensor.matmul(
+                        out=wasted[:],
+                        lhsT=k_side["raw"][:, 0, g, 2 * u, :P],
+                        rhs=k_side["raw"][:, 0, g, 2 * u, :],
+                        start=True,
+                        stop=True,
+                    )
 
         first = w_stage.tile([P, PASSES, K_PASS, PACK], BF16, name="w_grouped", align_bytes=64)
         lay_out_weight(nc.vector.tensor_copy, k_side, first, 0, 0, 0, K_PASS)

@@ -16,6 +16,7 @@ POS = 1024
 FEAT = 1024
 PASSES = FEAT // K_PASS
 BLOCKS = POS // P
+PAIRS = BLOCKS // 2
 GROUP = 512
 GROUPS = POS // GROUP
 BLOCKS_PER_GROUP = GROUP // P
@@ -80,13 +81,13 @@ def project_block(nc, psum, side, pe_mx, g2, block, grouped, i, copy):
     for t in range(PACK):
         w_cols = slice(t * P, (t + 1) * P)
         for g in range(PASSES):
-            pe_cols = slice(g * P, (g + 1) * P)
+            pe_cols = slice((block % 2) * P, (block % 2 + 1) * P)
             nc.tensor.matmul_mx(
                 out=bank[:, t, :],
                 lhsT=side["w_codes"][:, g2, g, w_cols].bitcast(FP8X4),
                 lhsT_scale=side["w_scales"][:, g2, g, w_cols],
-                rhs=pe_codes[:, block, pe_cols].bitcast(FP8X4),
-                rhs_scale=pe_scales[:, block, pe_cols],
+                rhs=pe_codes[:, block // 2, g, pe_cols].bitcast(FP8X4),
+                rhs_scale=pe_scales[:, block // 2, g, pe_cols],
                 start=(g == 0),
                 stop=(g == PASSES - 1),
             )
@@ -116,10 +117,10 @@ def tile_multiheadattention_tupe_pa_kernel(tc, pe, Uq, Uk, out):
         q_side = new_side(keep, "q")
         load_weight_half(nc, k_side, Uk, 0)
         pe_raw = keep.tile([P, BLOCKS * FEAT], BF16)
-        for pair in range(BLOCKS // 2):
+        for pair in range(PAIRS):
             nc.sync.dma_start(
-                out=pe_raw[:, 2 * pair * FEAT : 2 * (pair + 1) * FEAT].rearrange("p (r f) -> p r f", r=2),
-                in_=pe[2 * pair * P : 2 * (pair + 1) * P, :].rearrange("(r p) f -> p r f", p=P),
+                out=pe_raw[:, 2 * pair * FEAT : 2 * (pair + 1) * FEAT],
+                in_=pe[2 * pair * P : 2 * (pair + 1) * P, :].rearrange("(p r) f -> p (r f)", r=2),
             )
         load_weight_half(nc, k_side, Uk, 1)
         load_weight_half(nc, q_side, Uq, 0)
@@ -155,27 +156,29 @@ def tile_multiheadattention_tupe_pa_kernel(tc, pe, Uq, Uk, out):
         pe_words = pe_raw[:].bitcast(F32)
         pe_grouped = keep.tile([P, BLOCKS * PASSES * P * PACK], BF16, align_bytes=64)
         pe_grouped_words = pe_grouped[:].bitcast(F32).rearrange(
-            "p (r g c u) -> p r g c u", r=BLOCKS, g=PASSES, c=P
+            "p (j g c r u) -> p j g c r u", j=PAIRS, g=PASSES, c=P, r=2
         )
-        pe_codes = keep.tile([P, BLOCKS, PASSES * P], U32, align_bytes=64)
-        pe_scales = keep.tile([P, BLOCKS, PASSES * P], U8, align_bytes=64)
+        pe_codes = keep.tile([P, PAIRS, PASSES, 2 * P], U32, align_bytes=64)
+        pe_scales = keep.tile([P, PAIRS, PASSES, 2 * P], U8, align_bytes=64)
         pe_mx = (pe_codes, pe_scales)
         words_per_block = FEAT // 2
-        block_cols = PASSES * P * PACK
+        chunk_cols = 2 * P * PACK
 
-        def flip(r):
+        def flip(step):
+            j, g = divmod(step, PASSES)
             flipped = psum.tile([P, PACK, P], F32, tag="bank", name="flipped")
-            for w in range(PACK):
-                start = r * words_per_block + w * P
-                nc.tensor.transpose(flipped[:, w, :], pe_words[:, start : start + P], ident[:])
+            for r in range(2):
+                for u in range(2):
+                    start = (2 * j + r) * words_per_block + (2 * g + u) * P
+                    nc.tensor.transpose(flipped[:, 2 * r + u, :], pe_words[:, start : start + P], ident[:])
             nc.scalar.copy(
-                out=pe_grouped_words[:, r, :, :, :],
-                in_=flipped[:].rearrange("p (g u) c -> p g c u", u=2),
+                out=pe_grouped_words[:, j, g, :, :, :],
+                in_=flipped[:].rearrange("p (r u) c -> p c r u", u=2),
             )
             nc.vector.quantize_mx(
-                out=pe_codes[:, r, :].bitcast(FP8X4),
-                scales=pe_scales[:, r, :],
-                in_=pe_grouped[:, r * block_cols : (r + 1) * block_cols],
+                out=pe_codes[:, j, g, :].bitcast(FP8X4),
+                scales=pe_scales[:, j, g, :],
+                in_=pe_grouped[:, step * chunk_cols : (step + 1) * chunk_cols],
             )
 
         grouped_of = {}

@@ -193,6 +193,8 @@ def tile_multiheadattention_tupe_pa_kernel(tc, pe, Uq, Uk, out):
         second = w_stage.tile([P, PASSES, K_PASS, PACK], BF16, name="w_grouped", align_bytes=64)
         for r in range(BLOCKS):
             flip(r)
+            if r % 2 == 1 and r < BLOCKS - 1:
+                nc.tensor.matmul(out=wasted[:], lhsT=zeros[:, :P], rhs=zeros[:], start=True, stop=True)
             if r == C0_AFTER:
                 lay_out_weight(nc.vector.tensor_copy, k_side, second, 1, 0, 0, K_PASS)
             if r == C1_AFTER:

@@ -75,7 +75,7 @@ def quantise_weight_half(nc, stage, side, g2):
         quantise_weight(nc, side, grouped, g2, g)
 
 
-def project_block(nc, psum, side, pe_mx, g2, block, grouped, i, copy):
+def project_block(nc, psum, side, pe_mx, g2, block):
     pe_codes, pe_scales = pe_mx
     bank = psum.tile([P, PACK, P], F32, tag="bank", name="proj")
     for t in range(PACK):
@@ -91,6 +91,10 @@ def project_block(nc, psum, side, pe_mx, g2, block, grouped, i, copy):
                 start=(g == 0),
                 stop=(g == PASSES - 1),
             )
+    return bank
+
+
+def empty_bank(copy, bank, grouped, i):
     copy(out=grouped[:, i * P : (i + 1) * P, :], in_=bank[:].rearrange("p t c -> p c t"))
 
 
@@ -182,19 +186,24 @@ def tile_multiheadattention_tupe_pa_kernel(tc, pe, Uq, Uk, out):
             )
 
         grouped_of = {}
+        early_banks = {}
 
         def project(s, block):
             side, g2 = halves[s]
             h, i = divmod(block, BLOCKS_PER_GROUP)
             if i == 0:
                 grouped_of[(s, h)] = a_stage.tile([P, GROUP, PACK], BF16, tag="a_grouped4", name="a_grouped", align_bytes=64)
-            project_block(nc, psum, side, pe_mx, g2, block, grouped_of[(s, h)], i, nc.scalar.copy)
+            if (s, block) not in early_banks:
+                early_banks[(s, block)] = project_block(nc, psum, side, pe_mx, g2, block)
+            empty_bank(nc.scalar.copy, early_banks[(s, block)], grouped_of[(s, h)], i)
 
         second = w_stage.tile([P, PASSES, K_PASS, PACK], BF16, name="w_grouped", align_bytes=64)
         for r in range(BLOCKS):
             flip(r)
-            if r % 2 == 1 and r < BLOCKS - 1:
+            if r in (1, 3):
                 nc.tensor.matmul(out=wasted[:], lhsT=zeros[:, :P], rhs=zeros[:], start=True, stop=True)
+            if r == 5:
+                early_banks[(0, 0)] = project_block(nc, psum, k_side, pe_mx, 0, 0)
             if r == C0_AFTER:
                 lay_out_weight(nc.vector.tensor_copy, k_side, second, 1, 0, 0, K_PASS)
             if r == C1_AFTER:
@@ -220,7 +229,7 @@ def tile_multiheadattention_tupe_pa_kernel(tc, pe, Uq, Uk, out):
 
         def last_projection(n):
             grouped = a_stage.tile([P, P, PACK], BF16, tag="a_grouped1", name="a_grouped", align_bytes=64)
-            project_block(nc, psum, q_side, pe_mx, 1, n, grouped, 0, nc.scalar.copy)
+            empty_bank(nc.scalar.copy, project_block(nc, psum, q_side, pe_mx, 1, n), grouped, 0)
             quantise_projection(nc, q_side, grouped, 1, n, 1)
 
         def score(n):

from contextlib import ExitStack

import concourse.mybir as mybir
from concourse.masks import make_identity

BF16 = mybir.dt.bfloat16
F32 = mybir.dt.float32
U32 = mybir.dt.uint32
U8 = mybir.dt.uint8
FP8X4 = mybir.dt.float8_e4m3fn_x4

P = 128
PACK = 4
K_PASS = P * PACK
POS = 1024
FEAT = 1024
PASSES = FEAT // K_PASS
BLOCKS = POS // P
PAIRS = BLOCKS // 2
GROUP = 512
GROUPS = POS // GROUP
BLOCKS_PER_GROUP = GROUP // P
LEAD = 4
C0_AFTER = 5
C1_AFTER = 7
S_SHARE2 = 128
S_AT = 3
IDLE_WARMERS = 6
PIECE_WARMERS = 2

FLOPS = 3 * 2 * POS * FEAT * FEAT


def new_side(keep, label):
    return {
        "raw": keep.tile([P, PASSES, PASSES, PACK, K_PASS], BF16, name="%s_raw" % label),
        "w_codes": keep.tile([P, PASSES, PASSES, K_PASS], U32, name="%s_w_codes" % label, align_bytes=64),
        "w_scales": keep.tile([P, PASSES, PASSES, K_PASS], U8, name="%s_w_scales" % label, align_bytes=64),
        "codes": keep.tile([P, PASSES, POS], U32, name="%s_codes" % label, align_bytes=64),
        "scales": keep.tile([P, PASSES, POS], U8, name="%s_scales" % label, align_bytes=64),
    }


def load_weight_half(nc, side, weight, g2):
    cols = slice(g2 * K_PASS, (g2 + 1) * K_PASS)
    for g in range(PASSES):
        for u in range(2):
            first = g * K_PASS + u * 2 * P
            nc.sync.dma_start(
                out=side["raw"][:, g2, g, 2 * u : 2 * u + 2, :],
                in_=weight[first : first + 2 * P, cols].rearrange("(p e) c -> p e c", e=2),
            )


def lay_out_weight(engine_copy, side, grouped, g2, g, c0, c1):
    engine_copy(
        out=grouped[:, g, c0:c1, :].rearrange("p (c i) t -> p c t i", i=4),
        in_=side["raw"][:, g2, g, :, c0:c1].rearrange("p t (c i) -> p c t i", i=4),
    )


def quantise_weight(nc, side, grouped, g2, g):
    nc.vector.quantize_mx(
        out=side["w_codes"][:, g2, g, :].bitcast(FP8X4),
        scales=side["w_scales"][:, g2, g, :],
        in_=grouped[:, g, :, :].rearrange("p c t -> p (c t)"),
    )


def quantise_weight_half(nc, stage, side, g2):
    grouped = stage.tile([P, PASSES, K_PASS, PACK], BF16, name="w_grouped", align_bytes=64)
    for g in range(PASSES):
        lay_out_weight(nc.vector.tensor_copy, side, grouped, g2, g, 0, K_PASS)
    for g in range(PASSES):
        quantise_weight(nc, side, grouped, g2, g)


def project_block(nc, psum, side, pe_mx, g2, block):
    pe_codes, pe_scales = pe_mx
    bank = psum.tile([P, PACK, P], F32, tag="bank", name="proj")
    for t in range(PACK):
        w_cols = slice(t * P, (t + 1) * P)
        for g in range(PASSES):
            pe_cols = slice((block % 2) * P, (block % 2 + 1) * P)
            nc.tensor.matmul_mx(
                out=bank[:, t, :],
                lhsT=side["w_codes"][:, g2, g, w_cols].bitcast(FP8X4),
                lhsT_scale=side["w_scales"][:, g2, g, w_cols],
                rhs=pe_codes[:, block // 2, g, pe_cols].bitcast(FP8X4),
                rhs_scale=pe_scales[:, block // 2, g, pe_cols],
                start=(g == 0),
                stop=(g == PASSES - 1),
            )
    return bank


def empty_bank(copy, bank, grouped, i):
    copy(out=grouped[:, i * P : (i + 1) * P, :], in_=bank[:].rearrange("p t c -> p c t"))


def quantise_projection(nc, side, grouped, g2, first_block, n_blocks):
    cols = slice(first_block * P, (first_block + n_blocks) * P)
    nc.vector.quantize_mx(
        out=side["codes"][:, g2, cols].bitcast(FP8X4),
        scales=side["scales"][:, g2, cols],
        in_=grouped[:].rearrange("p c t -> p (c t)"),
    )


def tile_multiheadattention_tupe_pa_kernel(tc, pe, Uq, Uk, out):
    nc = tc.nc
    with ExitStack() as ctx:
        ctx.enter_context(tc.manual_schedule())
        keep = ctx.enter_context(tc.tile_pool(name="keep", bufs=1))
        w_stage = ctx.enter_context(tc.tile_pool(name="w_stage", bufs=2))
        a_stage = ctx.enter_context(tc.tile_pool(name="a_stage", bufs=6))
        rows_pool = ctx.enter_context(tc.tile_pool(name="rows_pool", bufs=3))
        psum = ctx.enter_context(tc.psum_pool(name="psum", bufs=8))

        k_side = new_side(keep, "k")
        q_side = new_side(keep, "q")
        load_weight_half(nc, k_side, Uk, 0)
        pe_raw = keep.tile([P, BLOCKS * FEAT], BF16)
        for pair in range(PAIRS):
            nc.sync.dma_start(
                out=pe_raw[:, 2 * pair * FEAT : 2 * (pair + 1) * FEAT],
                in_=pe[2 * pair * P : 2 * (pair + 1) * P, :].rearrange("(p r) f -> p (r f)", r=2),
            )
        load_weight_half(nc, k_side, Uk, 1)
        load_weight_half(nc, q_side, Uq, 0)
        load_weight_half(nc, q_side, Uq, 1)

        ident = keep.tile([P, P], F32)
        make_identity(nc, ident[:])

        halves = [(k_side, 0), (k_side, 1), (q_side, 0), (q_side, 1)]

        zeros = keep.tile([P, GROUP], BF16)
        nc.vector.memset(zeros[:], 0.0)
        wasted = psum.tile([P, GROUP], F32, tag="bank", name="wasted")
        for i in range(IDLE_WARMERS):
            nc.tensor.matmul(out=wasted[:], lhsT=zeros[:, :P], rhs=zeros[:], start=True, stop=True)
        for g in range(PASSES):
            for u in range(2):
                for i in range(PIECE_WARMERS):
                    nc.tensor.matmul(
                        out=wasted[:],
                        lhsT=k_side["raw"][:, 0, g, 2 * u, :P],
                        rhs=k_side["raw"][:, 0, g, 2 * u, :],
                        start=True,
                        stop=True,
                    )

        first = w_stage.tile([P, PASSES, K_PASS, PACK], BF16, name="w_grouped", align_bytes=64)
        lay_out_weight(nc.vector.tensor_copy, k_side, first, 0, 0, 0, K_PASS)
        lay_out_weight(nc.vector.tensor_copy, k_side, first, 0, 1, 0, K_PASS)
        quantise_weight(nc, k_side, first, 0, 0)
        quantise_weight(nc, k_side, first, 0, 1)

        pe_words = pe_raw[:].bitcast(F32)
        pe_grouped = keep.tile([P, BLOCKS * PASSES * P * PACK], BF16, align_bytes=64)
        pe_grouped_words = pe_grouped[:].bitcast(F32).rearrange(
            "p (j g c r u) -> p j g c r u", j=PAIRS, g=PASSES, c=P, r=2
        )
        pe_codes = keep.tile([P, PAIRS, PASSES, 2 * P], U32, align_bytes=64)
        pe_scales = keep.tile([P, PAIRS, PASSES, 2 * P], U8, align_bytes=64)
        pe_mx = (pe_codes, pe_scales)
        words_per_block = FEAT // 2
        chunk_cols = 2 * P * PACK

        def flip(step):
            j, g = divmod(step, PASSES)
            flipped = psum.tile([P, PACK, P], F32, tag="bank", name="flipped")
            for r in range(2):
                for u in range(2):
                    start = (2 * j + r) * words_per_block + (2 * g + u) * P
                    nc.tensor.transpose(flipped[:, 2 * r + u, :], pe_words[:, start : start + P], ident[:])
            nc.scalar.copy(
                out=pe_grouped_words[:, j, g, :, :, :],
                in_=flipped[:].rearrange("p (r u) c -> p c r u", u=2),
            )
            nc.vector.quantize_mx(
                out=pe_codes[:, j, g, :].bitcast(FP8X4),
                scales=pe_scales[:, j, g, :],
                in_=pe_grouped[:, step * chunk_cols : (step + 1) * chunk_cols],
            )

        grouped_of = {}
        early_banks = {}

        def project(s, block):
            side, g2 = halves[s]
            h, i = divmod(block, BLOCKS_PER_GROUP)
            if i == 0:
                grouped_of[(s, h)] = a_stage.tile([P, GROUP, PACK], BF16, tag="a_grouped4", name="a_grouped", align_bytes=64)
            if (s, block) not in early_banks:
                early_banks[(s, block)] = project_block(nc, psum, side, pe_mx, g2, block)
            empty_bank(nc.scalar.copy, early_banks[(s, block)], grouped_of[(s, h)], i)

        second = w_stage.tile([P, PASSES, K_PASS, PACK], BF16, name="w_grouped", align_bytes=64)
        for r in range(BLOCKS):
            flip(r)
            if r in (1, 3):
                nc.tensor.matmul(out=wasted[:], lhsT=zeros[:, :P], rhs=zeros[:], start=True, stop=True)
            if r == 5:
                early_banks[(0, 0)] = project_block(nc, psum, k_side, pe_mx, 0, 0)
            if r == C0_AFTER:
                lay_out_weight(nc.vector.tensor_copy, k_side, second, 1, 0, 0, K_PASS)
            if r == C1_AFTER:
                lay_out_weight(nc.vector.tensor_copy, k_side, second, 1, 1, 0, K_PASS - S_SHARE2)
        for block in range(S_AT):
            project(0, block)
        lay_out_weight(nc.scalar.copy, k_side, second, 1, 1, K_PASS - S_SHARE2, K_PASS)
        quantise_weight(nc, k_side, second, 1, 0)
        quantise_weight(nc, k_side, second, 1, 1)
        for side, g2 in halves[2:]:
            quantise_weight_half(nc, w_stage, side, g2)
        for block in range(S_AT, BLOCKS):
            project(0, block)
        for h in range(GROUPS):
            quantise_projection(nc, k_side, grouped_of[(0, h)], 0, h * BLOCKS_PER_GROUP, BLOCKS_PER_GROUP)
        for s in (1, 2):
            side, g2 = halves[s]
            for h in range(GROUPS):
                for i in range(BLOCKS_PER_GROUP):
                    project(s, h * BLOCKS_PER_GROUP + i)
                if (s, h) != (2, 1):
                    quantise_projection(nc, side, grouped_of[(s, h)], g2, h * BLOCKS_PER_GROUP, BLOCKS_PER_GROUP)

        def last_projection(n):
            grouped = a_stage.tile([P, P, PACK], BF16, tag="a_grouped1", name="a_grouped", align_bytes=64)
            empty_bank(nc.scalar.copy, project_block(nc, psum, q_side, pe_mx, 1, n), grouped, 0)
            quantise_projection(nc, q_side, grouped, 1, n, 1)

        def score(n):
            for h in range(GROUPS):
                scores = psum.tile([P, GROUP], F32, tag="bank", name="scores")
                keys = slice(h * GROUP, (h + 1) * GROUP)
                for g2 in range(PASSES):
                    nc.tensor.matmul_mx(
                        out=scores[:],
                        lhsT=q_side["codes"][:, g2, n * P : (n + 1) * P].bitcast(FP8X4),
                        lhsT_scale=q_side["scales"][:, g2, n * P : (n + 1) * P],
                        rhs=k_side["codes"][:, g2, keys].bitcast(FP8X4),
                        rhs_scale=k_side["scales"][:, g2, keys],
                        start=(g2 == 0),
                        stop=(g2 == PASSES - 1),
                    )
                rows = rows_pool.tile([P, GROUP], F32, tag="rows%d" % (h % 2), name="rows")
                if h % 2 == 0:
                    nc.vector.tensor_copy(out=rows[:], in_=scores[:])
                else:
                    nc.scalar.copy(out=rows[:], in_=scores[:])
                nc.sync.dma_start(out=out[n * P : (n + 1) * P, keys], in_=rows[:])

        for n in range(LEAD):
            last_projection(n)
        scored = 0
        for n in range(LEAD, BLOCKS + 1):
            for i in range(min(2, n - scored - 1) if n < BLOCKS else BLOCKS - scored):
                score(scored)
                if scored == 0:
                    quantise_projection(nc, q_side, grouped_of[(2, 1)], 0, BLOCKS_PER_GROUP, BLOCKS_PER_GROUP)
                scored += 1
            if n < BLOCKS:
                last_projection(n)
